import numpy as np
import ml_dtypes


def mxq(x, axis, fmt="e4m3"):
    dtype, down = {"e4m3": (ml_dtypes.float8_e4m3fn, 7), "e5m2": (ml_dtypes.float8_e5m2, 14)}[fmt]
    v = np.moveaxis(np.asarray(x, np.float32).astype(ml_dtypes.bfloat16).astype(np.float64), axis, -1)
    blocks = v.reshape(v.shape[:-1] + (-1, 32))
    amax = np.abs(blocks).max(-1, keepdims=True)
    byte = np.maximum(np.where(amax > 0, np.frexp(amax)[1] - 1 + 127, 0) - down, 1)
    scale = np.exp2(byte - 127.0)
    codes = (blocks / scale).astype(np.float32).astype(dtype).astype(np.float64)
    return np.moveaxis((codes * scale).reshape(v.shape), -1, axis)


WIDE = False


def mx_kscale(k):
    if not WIDE:
        return np.ones(k)
    levels = np.array([10, -10, 5, -5, 0])
    a = np.random.permutation(np.resize(levels, k // 512 * 4)).reshape(k // 512, 4)
    idx = np.arange(k)
    return np.exp2(a[idx // 512, idx % 128 // 32])


BF16 = ml_dtypes.bfloat16


def bf(x):
    return np.asarray(x, np.float32).astype(BF16)


def f64(x):
    return np.asarray(x).astype(np.float64)


E2M1 = np.array([0.0, 0.5, 1.0, 1.5, 2.0, 3.0, 4.0, 6.0, -0.0, -0.5, -1.0, -1.5, -2.0, -3.0, -4.0, -6.0])


def pack_weight(w, fmt):
    k, n = w.shape
    w = f64(bf(w)).reshape(k // 32, 32, n)
    amax = np.abs(w).max(1)
    if fmt == "e4m3":
        byte = np.frexp(amax)[1] - 1 + 127 - 7
    else:
        mant, ex = np.frexp(amax / 6.0)
        byte = np.where(mant > 0.5, ex, ex - 1) + 127
    byte = np.clip(np.where(amax > 0, byte, 1), 1, 254)
    scaled = (w * np.exp2(127.0 - byte)[:, None, :]).reshape(k, n).astype(np.float32)
    by_word = np.ascontiguousarray(scaled.reshape(k // 512, 128, 4, n).transpose(0, 1, 3, 2))
    if fmt == "e4m3":
        words = by_word.astype(ml_dtypes.float8_e4m3fn).view(np.uint8)
    else:
        c = by_word.astype(ml_dtypes.float4_e2m1fn).view(np.uint8) & 0xF
        words = c[..., 0::2] | (c[..., 1::2] << 4)
    return np.ascontiguousarray(words), np.ascontiguousarray(byte.astype(np.uint8).reshape(k // 512, 16, n))


def unpack_weight(words, scales, fmt):
    g, p, n, _ = words.shape
    if fmt == "e4m3":
        vals = np.ascontiguousarray(words).view(ml_dtypes.float8_e4m3fn).astype(np.float64)
    else:
        nib = np.empty((g, p, n, 4), np.uint8)
        nib[..., 0::2] = words & 0xF
        nib[..., 1::2] = words >> 4
        vals = E2M1[nib]
    vals = vals * np.repeat(np.exp2(scales.astype(np.float64) - 127.0), 8, axis=1)[..., None]
    return vals.transpose(0, 1, 3, 2).reshape(g * 512, n)


B, S, IN_DIM, UNITS = 1, 128, 4096, 4096
EPS = 1e-6
FMT = "e4m3"


def _ternary_kernel():
    limit = np.sqrt(6.0 / (IN_DIM + UNITS))
    w = np.random.uniform(-limit, limit, (IN_DIM, UNITS))
    scale = np.mean(np.abs(w)) + EPS
    return np.clip(np.round(w / scale), -1.0, 1.0)


def setup_inputs():
    s = mx_kscale(IN_DIM)
    x = bf(np.random.standard_normal((B, S, IN_DIM)) * (1.2 / np.sqrt(IN_DIM)) * s)
    words, scales = pack_weight(_ternary_kernel() / s[:, None], FMT)
    bias = bf(np.random.standard_normal(UNITS) * 0.1)
    return {"x": x, "kernel_words": words, "kernel_scales": scales, "bias": bias}


def reference(x, kernel_words, kernel_scales, bias):
    return (mxq(f64(x), 2, "e4m3") @ unpack_weight(kernel_words, kernel_scales, FMT)) + f64(bias)

@@ -1,0 +1,108 @@
+import concourse.mybir as mybir
+from concourse.masks import make_identity
+
+F32 = mybir.dt.float32
+BF16 = mybir.dt.bfloat16
+I32 = mybir.dt.int32
+U32 = mybir.dt.uint32
+U8 = mybir.dt.uint8
+FP8X4 = mybir.dt.float8_e4m3fn_x4
+
+P = 128
+K = 4096
+N = 4096
+G = K // 512
+NC = 512
+C = N // NC
+FLOPS = 2 * 128 * K * N
+
+
+def tile_bitlinear_w_kernel(tc, x, kernel_words, kernel_scales, bias, out):
+    nc = tc.nc
+    x2 = x.flatten_outer_dims()
+    out2 = out.flatten_outer_dims()
+    with tc.tile_pool(name="keep", bufs=1) as keep, tc.psum_pool(name="psum", bufs=1) as psum:
+        x_sb = keep.tile([P, K], BF16, align_bytes=64)
+        planes = [keep.tile([P, N], U8, name="planes%d" % j, align_bytes=64) for j in range(2)]
+        bias_rows = keep.tile([P, NC], BF16)
+        ident = keep.tile([P, P], F32)
+        ident_bf = keep.tile([P, C], BF16)
+        x_codes = keep.tile([P, G * P], U32, align_bytes=64)
+        x_plane = keep.tile([P, G * P], U8, align_bytes=64)
+        w_full = [keep.tile([P, N], U32, name="w%d" % g, align_bytes=64) for g in range(G - 1)]
+        w_last = [keep.tile([P, NC], U32, name="wl%d" % c, align_bytes=64) for c in range(C)]
+        bias_bc = [keep.tile([P, NC], F32, name="bb%d" % c) for c in range(C)]
+        out_sb = [keep.tile([P, NC], F32, name="o%d" % c) for c in range(C)]
+
+        nc.sync.dma_start(out=x_sb[:], in_=x2)
+        for j in range(2):
+            nc.vector.memset(planes[j][:].bitcast(I32), 0)
+        nc.vector.memset(bias_rows[:], 0.0)
+        make_identity(nc, ident[:])
+        nc.scalar.dma_start(out=bias_rows[0:C, :], in_=bias.rearrange("(c n) -> c n", c=C))
+        for j in range(2):
+            for q in range(4):
+                nc.sync.dma_start(
+                    out=planes[j][32 * q : 32 * q + 16, :].bitcast(I32),
+                    in_=kernel_scales[4 * j : 4 * j + 4, 4 * q : 4 * q + 4, :].bitcast(I32),
+                )
+        for g in range(G - 1):
+            nc.sync.dma_start(
+                out=w_full[g][:].bitcast(I32),
+                in_=kernel_words[g].rearrange("p n t -> p (n t)").bitcast(I32),
+            )
+        for c in range(C):
+            nc.sync.dma_start(
+                out=w_last[c][:].bitcast(I32),
+                in_=kernel_words[G - 1, :, NC * c : NC * (c + 1), :].rearrange("p n t -> p (n t)").bitcast(I32),
+            )
+
+        x_words = x_sb[:].bitcast(F32)
+        for b in range(4):
+            xt = psum.tile([P, 4, P], F32, tag="bank%d" % b, name="xt%d" % b)
+            for i in range(4):
+                g = 2 * b + i // 2
+                u = i % 2
+                nc.tensor.transpose(xt[:, i, :], x_words[:, 256 * g + u : 256 * (g + 1) : 2], ident[:])
+            grouped = keep.tile([P, 8 * P], BF16, name="grouped%d" % b, align_bytes=64)
+            dst = grouped[:].bitcast(F32).rearrange("p (g r u) -> p g r u", g=2, u=2)
+            src = xt[:].rearrange("p (g u) r -> p g r u", g=2)
+            if b % 2 == 0:
+                nc.vector.tensor_copy(out=dst, in_=src)
+            else:
+                nc.scalar.copy(out=dst, in_=src)
+            nc.vector.quantize_mx(
+                out=x_codes[:, 256 * b : 256 * (b + 1)].bitcast(FP8X4),
+                scales=x_plane[:, 256 * b : 256 * (b + 1)],
+                in_=grouped[:],
+            )
+
+        nc.vector.tensor_copy(out=ident_bf[:], in_=ident[:, 0:C])
+        for c in range(C):
+            pb = psum.tile([P, NC], F32, tag="bank%d" % (4 + c % 4), name="pb%d" % c)
+            nc.tensor.matmul(
+                out=pb[:], lhsT=ident_bf[:, c : c + 1].to_broadcast([P, P]), rhs=bias_rows[:], start=True, stop=True
+            )
+            if c % 2 == 0:
+                nc.scalar.copy(out=bias_bc[c][:], in_=pb[:])
+            else:
+                nc.vector.tensor_copy(out=bias_bc[c][:], in_=pb[:])
+
+        acc = [psum.tile([P, NC], F32, tag="bank%d" % c, name="acc%d" % c) for c in range(C)]
+        for g in range(G):
+            k = 4 * (g % 4)
+            for c in range(C):
+                cols = slice(NC * c, NC * (c + 1))
+                rhs = w_full[g][:, cols] if g < G - 1 else w_last[c][:]
+                nc.tensor.matmul_mx(
+                    out=acc[c][:],
+                    lhsT=x_codes[:, P * g : P * (g + 1)].bitcast(FP8X4),
+                    lhsT_scale=x_plane[:, P * g : P * (g + 1)],
+                    rhs=rhs.bitcast(FP8X4),
+                    rhs_scale=planes[g // 4][k:P, cols],
+                    start=(g == 0),
+                    stop=(g == G - 1),
+                )
+        for c in range(C):
+            nc.vector.tensor_tensor(out=out_sb[c][:], in0=acc[c][:], in1=bias_bc[c][:], op=mybir.AluOpType.add)
+            nc.sync.dma_start(out=out2[:, NC * c : NC * (c + 1)], in_=out_sb[c][:])

@@ -41,10 +41,10 @@ def tile_bitlinear_w_kernel(tc, x, kernel_words, kernel_scales, bias, out):
         make_identity(nc, ident[:])
         nc.scalar.dma_start(out=bias_rows[0:C, :], in_=bias.rearrange("(c n) -> c n", c=C))
         for j in range(2):
-            for q in range(4):
-                nc.sync.dma_start(
-                    out=planes[j][32 * q : 32 * q + 16, :].bitcast(I32),
-                    in_=kernel_scales[4 * j : 4 * j + 4, 4 * q : 4 * q + 4, :].bitcast(I32),
+            for q in (0, 2, 1, 3):
+                nc.gpsimd.dma_start(
+                    out=planes[j][32 * q : 32 * q + 16, :].bitcast(F32),
+                    in_=kernel_scales[4 * j : 4 * j + 4, 4 * q : 4 * q + 4, :].bitcast(F32),
                 )
         for g in range(G - 1):
             nc.sync.dma_start(

@@ -14,6 +14,7 @@ N = 4096
 G = K // 512
 NC = 512
 C = N // NC
+H = N // 2
 FLOPS = 2 * 128 * K * N
 
 
@@ -29,10 +30,22 @@ def tile_bitlinear_w_kernel(tc, x, kernel_words, kernel_scales, bias, out):
         ident_bf = keep.tile([P, C], BF16)
         x_codes = keep.tile([P, G * P], U32, align_bytes=64)
         x_plane = keep.tile([P, G * P], U8, align_bytes=64)
-        w_full = [keep.tile([P, N], U32, name="w%d" % g, align_bytes=64) for g in range(G - 1)]
+        w_half = [[keep.tile([P, H], U32, name="w%d_%d" % (g, h), align_bytes=64) for h in range(2)] for g in range(G - 1)]
         w_last = [keep.tile([P, NC], U32, name="wl%d" % c, align_bytes=64) for c in range(C)]
         bias_bc = [keep.tile([P, NC], F32, name="bb%d" % c) for c in range(C)]
         out_sb = [keep.tile([P, NC], F32, name="o%d" % c) for c in range(C)]
+
+        def load_half(g, h):
+            nc.sync.dma_start(
+                out=w_half[g][h][:].bitcast(I32),
+                in_=kernel_words[g, :, H * h : H * (h + 1), :].rearrange("p n t -> p (n t)").bitcast(I32),
+            )
+
+        def load_last(c):
+            nc.sync.dma_start(
+                out=w_last[c][:].bitcast(I32),
+                in_=kernel_words[G - 1, :, NC * c : NC * (c + 1), :].rearrange("p n t -> p (n t)").bitcast(I32),
+            )
 
         nc.sync.dma_start(out=x_sb[:], in_=x2)
         for j in range(2):
@@ -40,22 +53,24 @@ def tile_bitlinear_w_kernel(tc, x, kernel_words, kernel_scales, bias, out):
         nc.vector.memset(bias_rows[:], 0.0)
         make_identity(nc, ident[:])
         nc.scalar.dma_start(out=bias_rows[0:C, :], in_=bias.rearrange("(c n) -> c n", c=C))
-        for j in range(2):
-            for q in (0, 2, 1, 3):
-                nc.gpsimd.dma_start(
-                    out=planes[j][32 * q : 32 * q + 16, :].bitcast(F32),
-                    in_=kernel_scales[4 * j : 4 * j + 4, 4 * q : 4 * q + 4, :].bitcast(F32),
-                )
-        for g in range(G - 1):
+        for q in range(4):
             nc.sync.dma_start(
-                out=w_full[g][:].bitcast(I32),
-                in_=kernel_words[g].rearrange("p n t -> p (n t)").bitcast(I32),
+                out=planes[0][32 * q : 32 * q + 16, :].bitcast(I32),
+                in_=kernel_scales[0 : 4, 4 * q : 4 * q + 4, :].bitcast(I32),
             )
-        for c in range(C):
+        for q in range(4):
             nc.sync.dma_start(
-                out=w_last[c][:].bitcast(I32),
-                in_=kernel_words[G - 1, :, NC * c : NC * (c + 1), :].rearrange("p n t -> p (n t)").bitcast(I32),
+                out=planes[1][32 * q : 32 * q + 16, :].bitcast(I32),
+                in_=kernel_scales[4 : 8, 4 * q : 4 * q + 4, :].bitcast(I32),
             )
+        for g in range(G - 2):
+            load_half(g, 0)
+            load_half(g, 1)
+
+        for h in range(2):
+            load_half(G - 2, h)
+            for c in range(4 * h, 4 * h + 4):
+                load_last(c)
 
         x_words = x_sb[:].bitcast(F32)
         for b in range(4):
@@ -89,20 +104,30 @@ def tile_bitlinear_w_kernel(tc, x, kernel_words, kernel_scales, bias, out):
                 nc.vector.tensor_copy(out=bias_bc[c][:], in_=pb[:])
 
         acc = [psum.tile([P, NC], F32, tag="bank%d" % c, name="acc%d" % c) for c in range(C)]
-        for g in range(G):
+
+        def mx_pass(g, c):
             k = 4 * (g % 4)
+            if g < G - 1:
+                rhs = w_half[g][c // 4][:, NC * (c % 4) : NC * (c % 4 + 1)]
+            else:
+                rhs = w_last[c][:]
+            nc.tensor.matmul_mx(
+                out=acc[c][:],
+                lhsT=x_codes[:, P * g : P * (g + 1)].bitcast(FP8X4),
+                lhsT_scale=x_plane[:, P * g : P * (g + 1)],
+                rhs=rhs.bitcast(FP8X4),
+                rhs_scale=planes[g // 4][k:P, NC * c : NC * (c + 1)],
+                start=(g == 0),
+                stop=(g == G - 1),
+            )
+
+        for g in range(G - 2):
             for c in range(C):
-                cols = slice(NC * c, NC * (c + 1))
-                rhs = w_full[g][:, cols] if g < G - 1 else w_last[c][:]
-                nc.tensor.matmul_mx(
-                    out=acc[c][:],
-                    lhsT=x_codes[:, P * g : P * (g + 1)].bitcast(FP8X4),
-                    lhsT_scale=x_plane[:, P * g : P * (g + 1)],
-                    rhs=rhs.bitcast(FP8X4),
-                    rhs_scale=planes[g // 4][k:P, cols],
-                    start=(g == 0),
-                    stop=(g == G - 1),
-                )
-        for c in range(C):
-            nc.vector.tensor_tensor(out=out_sb[c][:], in0=acc[c][:], in1=bias_bc[c][:], op=mybir.AluOpType.add)
-            nc.sync.dma_start(out=out2[:, NC * c : NC * (c + 1)], in_=out_sb[c][:])
+                mx_pass(g, c)
+        for h in range(2):
+            for c in range(4 * h, 4 * h + 4):
+                mx_pass(G - 2, c)
+            for c in range(4 * h, 4 * h + 4):
+                mx_pass(G - 1, c)
+                nc.vector.tensor_tensor(out=out_sb[c][:], in0=acc[c][:], in1=bias_bc[c][:], op=mybir.AluOpType.add)
+                nc.sync.dma_start(out=out2[:, NC * c : NC * (c + 1)], in_=out_sb[c][:])

@@ -14,8 +14,16 @@ N = 4096
 G = K // 512
 NC = 512
 C = N // NC
-H = N // 2
 FLOPS = 2 * 128 * K * N
+
+PIECES = [(g, 2048 * h, 2048) for g in range(G - 2) for h in range(2)] + [
+    (G - 2, 0, 2048),
+    (G - 1, 0, 2048),
+    (G - 2, 2048, 2048),
+    (G - 1, 2048, 1024),
+    (G - 1, 3072, 1024),
+]
+STORES = [(0, 2048), (2048, 1024), (3072, 1024)]
 
 
 def tile_bitlinear_w_kernel(tc, x, kernel_words, kernel_scales, bias, out):
@@ -30,22 +38,9 @@ def tile_bitlinear_w_kernel(tc, x, kernel_words, kernel_scales, bias, out):
         ident_bf = keep.tile([P, C], BF16)
         x_codes = keep.tile([P, G * P], U32, align_bytes=64)
         x_plane = keep.tile([P, G * P], U8, align_bytes=64)
-        w_half = [[keep.tile([P, H], U32, name="w%d_%d" % (g, h), align_bytes=64) for h in range(2)] for g in range(G - 1)]
-        w_last = [keep.tile([P, NC], U32, name="wl%d" % c, align_bytes=64) for c in range(C)]
+        w_piece = [keep.tile([P, n], U32, name="w%d_%d" % (g, n0), align_bytes=64) for (g, n0, n) in PIECES]
         bias_bc = [keep.tile([P, NC], F32, name="bb%d" % c) for c in range(C)]
-        out_sb = [keep.tile([P, NC], F32, name="o%d" % c) for c in range(C)]
-
-        def load_half(g, h):
-            nc.sync.dma_start(
-                out=w_half[g][h][:].bitcast(I32),
-                in_=kernel_words[g, :, H * h : H * (h + 1), :].rearrange("p n t -> p (n t)").bitcast(I32),
-            )
-
-        def load_last(c):
-            nc.sync.dma_start(
-                out=w_last[c][:].bitcast(I32),
-                in_=kernel_words[G - 1, :, NC * c : NC * (c + 1), :].rearrange("p n t -> p (n t)").bitcast(I32),
-            )
+        out_sb = [keep.tile([P, n], F32, name="o%d" % n0) for (n0, n) in STORES]
 
         nc.sync.dma_start(out=x_sb[:], in_=x2)
         for j in range(2):
@@ -63,14 +58,12 @@ def tile_bitlinear_w_kernel(tc, x, kernel_words, kernel_scales, bias, out):
                 out=planes[1][32 * q : 32 * q + 16, :].bitcast(I32),
                 in_=kernel_scales[4 : 8, 4 * q : 4 * q + 4, :].bitcast(I32),
             )
-        for g in range(G - 2):
-            load_half(g, 0)
-            load_half(g, 1)
+        for i, (g, n0, n) in enumerate(PIECES):
+            nc.sync.dma_start(
+                out=w_piece[i][:].bitcast(I32),
+                in_=kernel_words[g, :, n0 : n0 + n, :].rearrange("p n t -> p (n t)").bitcast(I32),
+            )
 
-        for h in range(2):
-            load_half(G - 2, h)
-            for c in range(4 * h, 4 * h + 4):
-                load_last(c)
 
         x_words = x_sb[:].bitcast(F32)
         for b in range(4):
@@ -104,30 +97,24 @@ def tile_bitlinear_w_kernel(tc, x, kernel_words, kernel_scales, bias, out):
                 nc.vector.tensor_copy(out=bias_bc[c][:], in_=pb[:])
 
         acc = [psum.tile([P, NC], F32, tag="bank%d" % c, name="acc%d" % c) for c in range(C)]
-
-        def mx_pass(g, c):
+        for i, (g, n0, n) in enumerate(PIECES):
             k = 4 * (g % 4)
-            if g < G - 1:
-                rhs = w_half[g][c // 4][:, NC * (c % 4) : NC * (c % 4 + 1)]
-            else:
-                rhs = w_last[c][:]
-            nc.tensor.matmul_mx(
-                out=acc[c][:],
-                lhsT=x_codes[:, P * g : P * (g + 1)].bitcast(FP8X4),
-                lhsT_scale=x_plane[:, P * g : P * (g + 1)],
-                rhs=rhs.bitcast(FP8X4),
-                rhs_scale=planes[g // 4][k:P, NC * c : NC * (c + 1)],
-                start=(g == 0),
-                stop=(g == G - 1),
-            )
-
-        for g in range(G - 2):
-            for c in range(C):
-                mx_pass(g, c)
-        for h in range(2):
-            for c in range(4 * h, 4 * h + 4):
-                mx_pass(G - 2, c)
-            for c in range(4 * h, 4 * h + 4):
-                mx_pass(G - 1, c)
-                nc.vector.tensor_tensor(out=out_sb[c][:], in0=acc[c][:], in1=bias_bc[c][:], op=mybir.AluOpType.add)
-                nc.sync.dma_start(out=out2[:, NC * c : NC * (c + 1)], in_=out_sb[c][:])
+            for m in range(0, n, NC):
+                c = (n0 + m) // NC
+                nc.tensor.matmul_mx(
+                    out=acc[c][:],
+                    lhsT=x_codes[:, P * g : P * (g + 1)].bitcast(FP8X4),
+                    lhsT_scale=x_plane[:, P * g : P * (g + 1)],
+                    rhs=w_piece[i][:, m : m + NC].bitcast(FP8X4),
+                    rhs_scale=planes[g // 4][k:P, n0 + m : n0 + m + NC],
+                    start=(g == 0),
+                    stop=(g == G - 1),
+                )
+            if g == G - 1:
+                s = STORES.index((n0, n))
+                for m in range(0, n, NC):
+                    c = (n0 + m) // NC
+                    nc.vector.tensor_tensor(
+                        out=out_sb[s][:, m : m + NC], in0=acc[c][:], in1=bias_bc[c][:], op=mybir.AluOpType.add
+                    )
+                nc.sync.dma_start(out=out2[:, n0 : n0 + n], in_=out_sb[s][:])

@@ -53,10 +53,10 @@ def tile_bitlinear_w_kernel(tc, x, kernel_words, kernel_scales, bias, out):
                 out=planes[0][32 * q : 32 * q + 16, :].bitcast(I32),
                 in_=kernel_scales[0 : 4, 4 * q : 4 * q + 4, :].bitcast(I32),
             )
-        for q in range(4):
-            nc.sync.dma_start(
-                out=planes[1][32 * q : 32 * q + 16, :].bitcast(I32),
-                in_=kernel_scales[4 : 8, 4 * q : 4 * q + 4, :].bitcast(I32),
+        for q in (0, 2, 1, 3):
+            nc.gpsimd.dma_start(
+                out=planes[1][32 * q : 32 * q + 16, :].bitcast(F32),
+                in_=kernel_scales[4 : 8, 4 * q : 4 * q + 4, :].bitcast(F32),
             )
         for i, (g, n0, n) in enumerate(PIECES):
             nc.sync.dma_start(

@@ -31,7 +31,7 @@ def tile_bitlinear_w_kernel(tc, x, kernel_words, kernel_scales, bias, out):
     x2 = x.flatten_outer_dims()
     out2 = out.flatten_outer_dims()
     with tc.tile_pool(name="keep", bufs=1) as keep, tc.psum_pool(name="psum", bufs=1) as psum:
-        x_sb = keep.tile([P, K], BF16, align_bytes=64)
+        x_sb = [keep.tile([P, K // 2], BF16, name="x%d" % h, align_bytes=64) for h in range(2)]
         planes = [keep.tile([P, N], U8, name="planes%d" % j, align_bytes=64) for j in range(2)]
         bias_rows = keep.tile([P, NC], BF16)
         ident = keep.tile([P, P], F32)
@@ -42,12 +42,13 @@ def tile_bitlinear_w_kernel(tc, x, kernel_words, kernel_scales, bias, out):
         bias_bc = [keep.tile([P, NC], F32, name="bb%d" % c) for c in range(C)]
         out_sb = [keep.tile([P, n], F32, name="o%d" % n0) for (n0, n) in STORES]
 
-        nc.sync.dma_start(out=x_sb[:], in_=x2)
+        nc.vector.memset(bias_rows[:], 0.0)
+        nc.scalar.dma_start(out=bias_rows[0:C, :], in_=bias.rearrange("(c n) -> c n", c=C))
+        for h in range(2):
+            nc.sync.dma_start(out=x_sb[h][:], in_=x2[:, (K // 2) * h : (K // 2) * (h + 1)])
+        make_identity(nc, ident[:])
         for j in range(2):
             nc.vector.memset(planes[j][:].bitcast(I32), 0)
-        nc.vector.memset(bias_rows[:], 0.0)
-        make_identity(nc, ident[:])
-        nc.scalar.dma_start(out=bias_rows[0:C, :], in_=bias.rearrange("(c n) -> c n", c=C))
         for q in range(4):
             nc.sync.dma_start(
                 out=planes[0][32 * q : 32 * q + 16, :].bitcast(I32),
@@ -65,13 +66,24 @@ def tile_bitlinear_w_kernel(tc, x, kernel_words, kernel_scales, bias, out):
             )
 
 
-        x_words = x_sb[:].bitcast(F32)
+        nc.vector.tensor_copy(out=ident_bf[:], in_=ident[:, 0:C])
+        for c in range(C):
+            pb = psum.tile([P, NC], F32, tag="bank%d" % c, name="pb%d" % c)
+            nc.tensor.matmul(
+                out=pb[:], lhsT=ident_bf[:, c : c + 1].to_broadcast([P, P]), rhs=bias_rows[:], start=True, stop=True
+            )
+            if c % 2 == 0:
+                nc.scalar.copy(out=bias_bc[c][:], in_=pb[:])
+            else:
+                nc.vector.tensor_copy(out=bias_bc[c][:], in_=pb[:])
+
+        x_words = [x_sb[h][:].bitcast(F32) for h in range(2)]
         for b in range(4):
             xt = psum.tile([P, 4, P], F32, tag="bank%d" % b, name="xt%d" % b)
             for i in range(4):
                 g = 2 * b + i // 2
                 u = i % 2
-                nc.tensor.transpose(xt[:, i, :], x_words[:, 256 * g + u : 256 * (g + 1) : 2], ident[:])
+                nc.tensor.transpose(xt[:, i, :], x_words[g // 4][:, 256 * (g % 4) + u : 256 * (g % 4 + 1) : 2], ident[:])
             grouped = keep.tile([P, 8 * P], BF16, name="grouped%d" % b, align_bytes=64)
             dst = grouped[:].bitcast(F32).rearrange("p (g r u) -> p g r u", g=2, u=2)
             src = xt[:].rearrange("p (g u) r -> p g r u", g=2)
@@ -84,17 +96,6 @@ def tile_bitlinear_w_kernel(tc, x, kernel_words, kernel_scales, bias, out):
                 scales=x_plane[:, 256 * b : 256 * (b + 1)],
                 in_=grouped[:],
             )
-
-        nc.vector.tensor_copy(out=ident_bf[:], in_=ident[:, 0:C])
-        for c in range(C):
-            pb = psum.tile([P, NC], F32, tag="bank%d" % (4 + c % 4), name="pb%d" % c)
-            nc.tensor.matmul(
-                out=pb[:], lhsT=ident_bf[:, c : c + 1].to_broadcast([P, P]), rhs=bias_rows[:], start=True, stop=True
-            )
-            if c % 2 == 0:
-                nc.scalar.copy(out=bias_bc[c][:], in_=pb[:])
-            else:
-                nc.vector.tensor_copy(out=bias_bc[c][:], in_=pb[:])
 
         acc = [psum.tile([P, NC], F32, tag="bank%d" % c, name="acc%d" % c) for c in range(C)]
         for i, (g, n0, n) in enumerate(PIECES):

@@ -49,16 +49,17 @@ def tile_bitlinear_w_kernel(tc, x, kernel_words, kernel_scales, bias, out):
         make_identity(nc, ident[:])
         for j in range(2):
             nc.vector.memset(planes[j][:].bitcast(I32), 0)
-        for q in range(4):
-            nc.sync.dma_start(
-                out=planes[0][32 * q : 32 * q + 16, :].bitcast(I32),
-                in_=kernel_scales[0 : 4, 4 * q : 4 * q + 4, :].bitcast(I32),
-            )
-        for q in (0, 2, 1, 3):
-            nc.gpsimd.dma_start(
-                out=planes[1][32 * q : 32 * q + 16, :].bitcast(F32),
-                in_=kernel_scales[4 : 8, 4 * q : 4 * q + 4, :].bitcast(F32),
-            )
+        for j in range(2):
+            for q in range(2):
+                nc.sync.dma_start(
+                    out=planes[j][32 * q : 32 * q + 16, :].bitcast(I32),
+                    in_=kernel_scales[4 * j : 4 * j + 4, 4 * q : 4 * q + 4, :].bitcast(I32),
+                )
+            for q in range(2, 4):
+                nc.scalar.dma_start(
+                    out=planes[j][32 * q : 32 * q + 16, :].bitcast(F32),
+                    in_=kernel_scales[4 * j : 4 * j + 4, 4 * q : 4 * q + 4, :].bitcast(F32),
+                )
         for i, (g, n0, n) in enumerate(PIECES):
             nc.sync.dma_start(
                 out=w_piece[i][:].bitcast(I32),

@@ -49,23 +49,25 @@ def tile_bitlinear_w_kernel(tc, x, kernel_words, kernel_scales, bias, out):
         make_identity(nc, ident[:])
         for j in range(2):
             nc.vector.memset(planes[j][:].bitcast(I32), 0)
+        def load_scales(queue, view, j, q, c0, c1):
+            queue.dma_start(
+                out=planes[j][32 * q : 32 * q + 16, c0:c1].bitcast(view),
+                in_=kernel_scales[4 * j : 4 * j + 4, 4 * q : 4 * q + 4, c0:c1].bitcast(view),
+            )
+
+        load_scales(nc.sync, I32, 0, 0, 0, N)
+        load_scales(nc.sync, I32, 0, 1, 0, N)
+        load_scales(nc.sync, I32, 1, 0, 0, N)
+        load_scales(nc.sync, I32, 1, 1, 0, N // 2)
+        load_scales(nc.sync, I32, 1, 1, N // 2, N)
         for j in range(2):
-            for q in range(2):
-                nc.sync.dma_start(
-                    out=planes[j][32 * q : 32 * q + 16, :].bitcast(I32),
-                    in_=kernel_scales[4 * j : 4 * j + 4, 4 * q : 4 * q + 4, :].bitcast(I32),
-                )
             for q in range(2, 4):
-                nc.scalar.dma_start(
-                    out=planes[j][32 * q : 32 * q + 16, :].bitcast(F32),
-                    in_=kernel_scales[4 * j : 4 * j + 4, 4 * q : 4 * q + 4, :].bitcast(F32),
-                )
+                load_scales(nc.scalar, F32, j, q, 0, N)
         for i, (g, n0, n) in enumerate(PIECES):
             nc.sync.dma_start(
                 out=w_piece[i][:].bitcast(I32),
                 in_=kernel_words[g, :, n0 : n0 + n, :].rearrange("p n t -> p (n t)").bitcast(I32),
             )
-
 
         nc.vector.tensor_copy(out=ident_bf[:], in_=ident[:, 0:C])
         for c in range(C):

@@ -47,7 +47,7 @@ def tile_bitlinear_w_kernel(tc, x, kernel_words, kernel_scales, bias, out):
         for h in range(2):
             nc.sync.dma_start(out=x_sb[h][:], in_=x2[:, (K // 2) * h : (K // 2) * (h + 1)])
         make_identity(nc, ident[:])
-        for j in range(2):
+        for j in (1, 0):
             nc.vector.memset(planes[j][:].bitcast(I32), 0)
         def load_scales(queue, view, j, q, c0, c1):
             queue.dma_start(
@@ -55,14 +55,14 @@ def tile_bitlinear_w_kernel(tc, x, kernel_words, kernel_scales, bias, out):
                 in_=kernel_scales[4 * j : 4 * j + 4, 4 * q : 4 * q + 4, c0:c1].bitcast(view),
             )
 
-        load_scales(nc.sync, I32, 0, 0, 0, N)
-        load_scales(nc.sync, I32, 0, 1, 0, N)
-        load_scales(nc.sync, I32, 1, 0, 0, N)
-        load_scales(nc.sync, I32, 1, 1, 0, N // 2)
-        load_scales(nc.sync, I32, 1, 1, N // 2, N)
-        for j in range(2):
-            for q in range(2, 4):
-                load_scales(nc.scalar, F32, j, q, 0, N)
+        for q in (0, 2, 1, 3):
+            load_scales(nc.gpsimd, F32, 1, q, 0, N)
+        for q in range(2):
+            for h in range(2):
+                load_scales(nc.sync, I32, 0, q, h * (N // 2), (h + 1) * (N // 2))
+        for q in range(2, 4):
+            for h in range(2):
+                load_scales(nc.scalar, F32, 0, q, h * (N // 2), (h + 1) * (N // 2))
         for i, (g, n0, n) in enumerate(PIECES):
             nc.sync.dma_start(
                 out=w_piece[i][:].bitcast(I32),

@@ -75,10 +75,7 @@ def tile_bitlinear_w_kernel(tc, x, kernel_words, kernel_scales, bias, out):
             nc.tensor.matmul(
                 out=pb[:], lhsT=ident_bf[:, c : c + 1].to_broadcast([P, P]), rhs=bias_rows[:], start=True, stop=True
             )
-            if c % 2 == 0:
-                nc.scalar.copy(out=bias_bc[c][:], in_=pb[:])
-            else:
-                nc.vector.tensor_copy(out=bias_bc[c][:], in_=pb[:])
+            nc.vector.tensor_copy(out=bias_bc[c][:], in_=pb[:])
 
         x_words = [x_sb[h][:].bitcast(F32) for h in range(2)]
         for b in range(4):
@@ -90,10 +87,7 @@ def tile_bitlinear_w_kernel(tc, x, kernel_words, kernel_scales, bias, out):
             grouped = keep.tile([P, 8 * P], BF16, name="grouped%d" % b, align_bytes=64)
             dst = grouped[:].bitcast(F32).rearrange("p (g r u) -> p g r u", g=2, u=2)
             src = xt[:].rearrange("p (g u) r -> p g r u", g=2)
-            if b % 2 == 0:
-                nc.vector.tensor_copy(out=dst, in_=src)
-            else:
-                nc.scalar.copy(out=dst, in_=src)
+            nc.vector.tensor_copy(out=dst, in_=src)
             nc.vector.quantize_mx(
                 out=x_codes[:, 256 * b : 256 * (b + 1)].bitcast(FP8X4),
                 scales=x_plane[:, 256 * b : 256 * (b + 1)],

import concourse.mybir as mybir
from concourse.masks import make_identity

F32 = mybir.dt.float32
BF16 = mybir.dt.bfloat16
I32 = mybir.dt.int32
U32 = mybir.dt.uint32
U8 = mybir.dt.uint8
FP8X4 = mybir.dt.float8_e4m3fn_x4

P = 128
K = 4096
N = 4096
G = K // 512
NC = 512
C = N // NC
FLOPS = 2 * 128 * K * N

PIECES = [(g, 2048 * h, 2048) for g in range(G - 2) for h in range(2)] + [
    (G - 2, 0, 2048),
    (G - 1, 0, 2048),
    (G - 2, 2048, 2048),
    (G - 1, 2048, 1024),
    (G - 1, 3072, 1024),
]
STORES = [(0, 2048), (2048, 1024), (3072, 1024)]


def tile_bitlinear_w_kernel(tc, x, kernel_words, kernel_scales, bias, out):
    nc = tc.nc
    x2 = x.flatten_outer_dims()
    out2 = out.flatten_outer_dims()
    with tc.tile_pool(name="keep", bufs=1) as keep, tc.psum_pool(name="psum", bufs=1) as psum:
        x_sb = [keep.tile([P, K // 2], BF16, name="x%d" % h, align_bytes=64) for h in range(2)]
        planes = [keep.tile([P, N], U8, name="planes%d" % j, align_bytes=64) for j in range(2)]
        bias_rows = keep.tile([P, NC], BF16)
        ident = keep.tile([P, P], F32)
        ident_bf = keep.tile([P, C], BF16)
        x_codes = keep.tile([P, G * P], U32, align_bytes=64)
        x_plane = keep.tile([P, G * P], U8, align_bytes=64)
        w_piece = [keep.tile([P, n], U32, name="w%d_%d" % (g, n0), align_bytes=64) for (g, n0, n) in PIECES]
        bias_bc = [keep.tile([P, NC], F32, name="bb%d" % c) for c in range(C)]
        out_sb = [keep.tile([P, n], F32, name="o%d" % n0) for (n0, n) in STORES]

        nc.vector.memset(bias_rows[:], 0.0)
        nc.scalar.dma_start(out=bias_rows[0:C, :], in_=bias.rearrange("(c n) -> c n", c=C))
        for h in range(2):
            nc.sync.dma_start(out=x_sb[h][:], in_=x2[:, (K // 2) * h : (K // 2) * (h + 1)])
        make_identity(nc, ident[:])
        for j in (1, 0):
            nc.vector.memset(planes[j][:].bitcast(I32), 0)
        def load_scales(queue, view, j, q, c0, c1):
            queue.dma_start(
                out=planes[j][32 * q : 32 * q + 16, c0:c1].bitcast(view),
                in_=kernel_scales[4 * j : 4 * j + 4, 4 * q : 4 * q + 4, c0:c1].bitcast(view),
            )

        for q in (0, 2, 1, 3):
            load_scales(nc.gpsimd, F32, 1, q, 0, N)
        for q in range(2):
            for h in range(2):
                load_scales(nc.sync, I32, 0, q, h * (N // 2), (h + 1) * (N // 2))
        for q in range(2, 4):
            for h in range(2):
                load_scales(nc.scalar, F32, 0, q, h * (N // 2), (h + 1) * (N // 2))
        for i, (g, n0, n) in enumerate(PIECES):
            nc.sync.dma_start(
                out=w_piece[i][:].bitcast(I32),
                in_=kernel_words[g, :, n0 : n0 + n, :].rearrange("p n t -> p (n t)").bitcast(I32),
            )

        nc.vector.tensor_copy(out=ident_bf[:], in_=ident[:, 0:C])
        for c in range(C):
            pb = psum.tile([P, NC], F32, tag="bank%d" % c, name="pb%d" % c)
            nc.tensor.matmul(
                out=pb[:], lhsT=ident_bf[:, c : c + 1].to_broadcast([P, P]), rhs=bias_rows[:], start=True, stop=True
            )
            nc.vector.tensor_copy(out=bias_bc[c][:], in_=pb[:])

        x_words = [x_sb[h][:].bitcast(F32) for h in range(2)]
        for b in range(4):
            xt = psum.tile([P, 4, P], F32, tag="bank%d" % b, name="xt%d" % b)
            for i in range(4):
                g = 2 * b + i // 2
                u = i % 2
                nc.tensor.transpose(xt[:, i, :], x_words[g // 4][:, 256 * (g % 4) + u : 256 * (g % 4 + 1) : 2], ident[:])
            grouped = keep.tile([P, 8 * P], BF16, name="grouped%d" % b, align_bytes=64)
            dst = grouped[:].bitcast(F32).rearrange("p (g r u) -> p g r u", g=2, u=2)
            src = xt[:].rearrange("p (g u) r -> p g r u", g=2)
            nc.vector.tensor_copy(out=dst, in_=src)
            nc.vector.quantize_mx(
                out=x_codes[:, 256 * b : 256 * (b + 1)].bitcast(FP8X4),
                scales=x_plane[:, 256 * b : 256 * (b + 1)],
                in_=grouped[:],
            )

        acc = [psum.tile([P, NC], F32, tag="bank%d" % c, name="acc%d" % c) for c in range(C)]
        for i, (g, n0, n) in enumerate(PIECES):
            k = 4 * (g % 4)
            for m in range(0, n, NC):
                c = (n0 + m) // NC
                nc.tensor.matmul_mx(
                    out=acc[c][:],
                    lhsT=x_codes[:, P * g : P * (g + 1)].bitcast(FP8X4),
                    lhsT_scale=x_plane[:, P * g : P * (g + 1)],
                    rhs=w_piece[i][:, m : m + NC].bitcast(FP8X4),
                    rhs_scale=planes[g // 4][k:P, n0 + m : n0 + m + NC],
                    start=(g == 0),
                    stop=(g == G - 1),
                )
            if g == G - 1:
                s = STORES.index((n0, n))
                for m in range(0, n, NC):
                    c = (n0 + m) // NC
                    nc.vector.tensor_tensor(
                        out=out_sb[s][:, m : m + NC], in0=acc[c][:], in1=bias_bc[c][:], op=mybir.AluOpType.add
                    )
                nc.sync.dma_start(out=out2[:, n0 : n0 + n], in_=out_sb[s][:])
